import numpy as np
import ml_dtypes

BF16 = ml_dtypes.bfloat16


def bf(x):
    return np.asarray(x, np.float32).astype(BF16)


def f32(x):
    return np.asarray(x, np.float32)


def f64(x):
    return np.asarray(x).astype(np.float64)


def striped(idx):
    return np.tile(idx.reshape(-1, 16).T, (8, 1))


D, H, Q, M, S, N = 128, 2, 128, 256, 1024, 512
SCALE = 1.0 / np.sqrt(D)


def setup_inputs():
    return {"table": bf(np.random.standard_normal((D, S))), "w": bf(0.5 * np.random.standard_normal((D, M))), "keys": bf(np.random.standard_normal((H * D, N))), "offs": striped(np.random.permutation(np.tile(np.arange(S), 2))[:N])}


def reference(table, w, keys, offs):
    idx = offs[:16].T.reshape(-1)
    rk = f64(table)[:, idx]
    rows = []
    for h in range(H):
        wq = f64(w)[:, h * Q:(h + 1) * Q]
        rows.append(wq.T @ f64(keys)[h * D:(h + 1) * D] + wq.T @ rk)
    return np.concatenate(rows, axis=0) * SCALE

@@ -1,0 +1,41 @@
+import math
+
+import concourse.mybir as mybir
+
+BF16, F32, U16 = mybir.dt.bfloat16, mybir.dt.float32, mybir.dt.uint16
+
+D = 128
+HEADS = 2
+Q = 128
+CODES = 1024
+N = 512
+SCALE = 1.0 / math.sqrt(D)
+
+FLOPS = 2 * 2 * HEADS * Q * D * N
+
+
+def tile_multiheadattention_shaw_kernel(tc, table, w, keys, offs, out):
+    nc = tc.nc
+    with (
+        tc.tile_pool(name="held", bufs=1) as held,
+        tc.psum_pool(name="psum", bufs=1) as psum,
+    ):
+        offsets = held.tile([D, N // 16], U16, name="offsets")
+        nc.sync.dma_start(offsets[:], offs)
+        queries = held.tile([D, HEADS * Q], BF16, name="queries")
+        nc.sync.dma_start(queries[:], w)
+        codes = held.tile([D, CODES], BF16, name="codes")
+        nc.sync.dma_start(codes[:], table)
+
+        for h in range(HEADS):
+            head_keys = held.tile([D, N], BF16, name=f"head_keys{h}")
+            nc.sync.dma_start(head_keys[:], keys[h * D : (h + 1) * D, :])
+            head_queries = queries[:, h * Q : (h + 1) * Q]
+
+            scores = psum.tile([Q, N], F32, name=f"scores{h}")
+            nc.tensor.matmul(scores[:], head_queries, codes[:].indirect(offsets[:]), start=True, stop=False)
+            nc.tensor.matmul(scores[:], head_queries, head_keys[:], start=False, stop=True)
+
+            scaled = held.tile([Q, N], F32, name=f"scaled{h}")
+            nc.vector.tensor_scalar_mul(scaled[:], scores[:], SCALE)
+            nc.sync.dma_start(out[h * Q : (h + 1) * Q, :], scaled[:])

@@ -3,6 +3,7 @@ import math
 import concourse.mybir as mybir
 
 BF16, F32, U16 = mybir.dt.bfloat16, mybir.dt.float32, mybir.dt.uint16
+COPY = mybir.ActivationFunctionType.Copy
 
 D = 128
 HEADS = 2
@@ -10,6 +11,8 @@ Q = 128
 CODES = 1024
 N = 512
 SCALE = 1.0 / math.sqrt(D)
+
+WARM_MATMULS = 4
 
 FLOPS = 2 * 2 * HEADS * Q * D * N
 
@@ -22,20 +25,29 @@ def tile_multiheadattention_shaw_kernel(tc, table, w, keys, offs, out):
     ):
         offsets = held.tile([D, N // 16], U16, name="offsets")
         nc.sync.dma_start(offsets[:], offs)
-        queries = held.tile([D, HEADS * Q], BF16, name="queries")
-        nc.sync.dma_start(queries[:], w)
         codes = held.tile([D, CODES], BF16, name="codes")
         nc.sync.dma_start(codes[:], table)
-
+        queries = held.tile([D, HEADS * Q], BF16, name="queries")
+        nc.scalar.dma_start(queries[:], w)
+        head_keys = [held.tile([D, N], BF16, name=f"head_keys{h}") for h in range(HEADS)]
         for h in range(HEADS):
-            head_keys = held.tile([D, N], BF16, name=f"head_keys{h}")
-            nc.sync.dma_start(head_keys[:], keys[h * D : (h + 1) * D, :])
-            head_queries = queries[:, h * Q : (h + 1) * Q]
+            nc.scalar.dma_start(head_keys[h][:], keys[h * D : (h + 1) * D, :])
 
-            scores = psum.tile([Q, N], F32, name=f"scores{h}")
-            nc.tensor.matmul(scores[:], head_queries, codes[:].indirect(offsets[:]), start=True, stop=False)
-            nc.tensor.matmul(scores[:], head_queries, head_keys[:], start=False, stop=True)
+        zeros = held.tile([D, N], BF16, name="zeros")
+        nc.vector.memset(zeros[:], 0.0)
+        unread = psum.tile([Q, N], F32, name="unread")
+        for i in range(WARM_MATMULS):
+            nc.tensor.matmul(unread[:], zeros[:, 0:Q], zeros[:], start=True, stop=True)
 
-            scaled = held.tile([Q, N], F32, name=f"scaled{h}")
-            nc.vector.tensor_scalar_mul(scaled[:], scores[:], SCALE)
-            nc.sync.dma_start(out[h * Q : (h + 1) * Q, :], scaled[:])
+        head_queries = [queries[:, h * Q : (h + 1) * Q] for h in range(HEADS)]
+        scores = [psum.tile([Q, N], F32, name=f"scores{h}") for h in range(HEADS)]
+        for h in range(HEADS):
+            nc.tensor.matmul(scores[h][:], head_queries[h], codes[:].indirect(offsets[:]), start=True, stop=False)
+        for h in range(HEADS):
+            nc.tensor.matmul(scores[h][:], head_queries[h], head_keys[h][:], start=False, stop=True)
+
+        scaled = [held.tile([Q, N], F32, name=f"scaled{h}") for h in range(HEADS)]
+        nc.vector.tensor_scalar_mul(scaled[0][:], scores[0][:], SCALE)
+        nc.sync.dma_start(out[0:Q, :], scaled[0][:])
+        nc.scalar.activation(scaled[1][:], scores[1][:], COPY, scale=SCALE)
+        nc.scalar.dma_start(out[Q : 2 * Q, :], scaled[1][:])

@@ -12,8 +12,6 @@ CODES = 1024
 N = 512
 SCALE = 1.0 / math.sqrt(D)
 
-WARM_MATMULS = 4
-
 FLOPS = 2 * 2 * HEADS * Q * D * N
 
 
@@ -32,12 +30,6 @@ def tile_multiheadattention_shaw_kernel(tc, table, w, keys, offs, out):
         head_keys = [held.tile([D, N], BF16, name=f"head_keys{h}") for h in range(HEADS)]
         for h in range(HEADS):
             nc.scalar.dma_start(head_keys[h][:], keys[h * D : (h + 1) * D, :])
-
-        zeros = held.tile([D, N], BF16, name="zeros")
-        nc.vector.memset(zeros[:], 0.0)
-        unread = psum.tile([Q, N], F32, name="unread")
-        for i in range(WARM_MATMULS):
-            nc.tensor.matmul(unread[:], zeros[:, 0:Q], zeros[:], start=True, stop=True)
 
         head_queries = [queries[:, h * Q : (h + 1) * Q] for h in range(HEADS)]
         scores = [psum.tile([Q, N], F32, name=f"scores{h}") for h in range(HEADS)]

@@ -10,6 +10,8 @@ HEADS = 2
 Q = 128
 CODES = 1024
 N = 512
+PIECE = 256
+PIECES = N // PIECE
 SCALE = 1.0 / math.sqrt(D)
 
 FLOPS = 2 * 2 * HEADS * Q * D * N
@@ -21,25 +23,40 @@ def tile_multiheadattention_shaw_kernel(tc, table, w, keys, offs, out):
         tc.tile_pool(name="held", bufs=1) as held,
         tc.psum_pool(name="psum", bufs=1) as psum,
     ):
+        queries = held.tile([D, HEADS * Q], BF16, name="queries")
+        nc.sync.dma_start(queries[:], w)
+        head_keys = [held.tile([D, N], BF16, name=f"head_keys{h}") for h in range(HEADS)]
+        for h in range(HEADS):
+            nc.sync.dma_start(head_keys[h][:], keys[h * D : (h + 1) * D, :])
         offsets = held.tile([D, N // 16], U16, name="offsets")
         nc.sync.dma_start(offsets[:], offs)
         codes = held.tile([D, CODES], BF16, name="codes")
         nc.sync.dma_start(codes[:], table)
-        queries = held.tile([D, HEADS * Q], BF16, name="queries")
-        nc.scalar.dma_start(queries[:], w)
-        head_keys = [held.tile([D, N], BF16, name=f"head_keys{h}") for h in range(HEADS)]
-        for h in range(HEADS):
-            nc.scalar.dma_start(head_keys[h][:], keys[h * D : (h + 1) * D, :])
 
-        head_queries = [queries[:, h * Q : (h + 1) * Q] for h in range(HEADS)]
-        scores = [psum.tile([Q, N], F32, name=f"scores{h}") for h in range(HEADS)]
-        for h in range(HEADS):
-            nc.tensor.matmul(scores[h][:], head_queries[h], codes[:].indirect(offsets[:]), start=True, stop=False)
-        for h in range(HEADS):
-            nc.tensor.matmul(scores[h][:], head_queries[h], head_keys[h][:], start=False, stop=True)
+        pieces = [(h, p) for h in range(HEADS) for p in range(PIECES)]
+        scores = [psum.tile([Q, PIECE], F32, name=f"scores{h}{p}") for h, p in pieces]
 
-        scaled = [held.tile([Q, N], F32, name=f"scaled{h}") for h in range(HEADS)]
-        nc.vector.tensor_scalar_mul(scaled[0][:], scores[0][:], SCALE)
-        nc.sync.dma_start(out[0:Q, :], scaled[0][:])
-        nc.scalar.activation(scaled[1][:], scores[1][:], COPY, scale=SCALE)
-        nc.scalar.dma_start(out[Q : 2 * Q, :], scaled[1][:])
+        for (h, p), bank in zip(pieces, scores):
+            nc.tensor.matmul(
+                bank[:],
+                queries[:, h * Q : (h + 1) * Q],
+                head_keys[h][:, p * PIECE : (p + 1) * PIECE],
+                start=True,
+                stop=False,
+            )
+
+        for i, ((h, p), bank) in enumerate(zip(pieces, scores)):
+            piece_offsets = offsets[:, p * (PIECE // 16) : (p + 1) * (PIECE // 16)]
+            nc.tensor.matmul(
+                bank[:],
+                queries[:, h * Q : (h + 1) * Q],
+                codes[:].indirect(piece_offsets),
+                start=False,
+                stop=True,
+            )
+            scaled = held.tile([Q, PIECE], F32, name=f"scaled{h}{p}")
+            if i % 2 == 0:
+                nc.vector.tensor_scalar_mul(scaled[:], bank[:], SCALE)
+            else:
+                nc.scalar.activation(scaled[:], bank[:], COPY, scale=SCALE)
+            nc.sync.dma_start(out[h * Q : (h + 1) * Q, p * PIECE : (p + 1) * PIECE], scaled[:])

@@ -13,6 +13,7 @@ N = 512
 PIECE = 256
 PIECES = N // PIECE
 SCALE = 1.0 / math.sqrt(D)
+WARM_MATMULS = 12
 
 FLOPS = 2 * 2 * HEADS * Q * D * N
 
@@ -32,6 +33,12 @@ def tile_multiheadattention_shaw_kernel(tc, table, w, keys, offs, out):
         nc.sync.dma_start(offsets[:], offs)
         codes = held.tile([D, CODES], BF16, name="codes")
         nc.sync.dma_start(codes[:], table)
+
+        zeros = held.tile([D, Q], BF16, name="zeros")
+        nc.vector.memset(zeros[:], 0.0)
+        unread = psum.tile([Q, Q], F32, name="unread")
+        for i in range(WARM_MATMULS):
+            nc.tensor.matmul(unread[:], zeros[:], zeros[:], start=True, stop=True)
 
         pieces = [(h, p) for h in range(HEADS) for p in range(PIECES)]
         scores = [psum.tile([Q, PIECE], F32, name=f"scores{h}{p}") for h, p in pieces]

@@ -10,10 +10,8 @@ HEADS = 2
 Q = 128
 CODES = 1024
 N = 512
-PIECE = 256
-PIECES = N // PIECE
+WIDTHS = ((256, 256), (128, 128, 128, 128))
 SCALE = 1.0 / math.sqrt(D)
-WARM_MATMULS = 12
 
 FLOPS = 2 * 2 * HEADS * Q * D * N
 
@@ -34,36 +32,29 @@ def tile_multiheadattention_shaw_kernel(tc, table, w, keys, offs, out):
         codes = held.tile([D, CODES], BF16, name="codes")
         nc.sync.dma_start(codes[:], table)
 
-        zeros = held.tile([D, Q], BF16, name="zeros")
-        nc.vector.memset(zeros[:], 0.0)
-        unread = psum.tile([Q, Q], F32, name="unread")
-        for i in range(WARM_MATMULS):
-            nc.tensor.matmul(unread[:], zeros[:], zeros[:], start=True, stop=True)
+        pieces = [(h, sum(WIDTHS[h][:p]), WIDTHS[h][p]) for h in range(HEADS) for p in range(len(WIDTHS[h]))]
+        scores = [psum.tile([Q, width], F32, name=f"scores{h}_{first}") for h, first, width in pieces]
 
-        pieces = [(h, p) for h in range(HEADS) for p in range(PIECES)]
-        scores = [psum.tile([Q, PIECE], F32, name=f"scores{h}{p}") for h, p in pieces]
-
-        for (h, p), bank in zip(pieces, scores):
+        for (h, first, width), bank in zip(pieces, scores):
             nc.tensor.matmul(
                 bank[:],
                 queries[:, h * Q : (h + 1) * Q],
-                head_keys[h][:, p * PIECE : (p + 1) * PIECE],
+                head_keys[h][:, first : first + width],
                 start=True,
                 stop=False,
             )
 
-        for i, ((h, p), bank) in enumerate(zip(pieces, scores)):
-            piece_offsets = offsets[:, p * (PIECE // 16) : (p + 1) * (PIECE // 16)]
+        for i, ((h, first, width), bank) in enumerate(zip(pieces, scores)):
             nc.tensor.matmul(
                 bank[:],
                 queries[:, h * Q : (h + 1) * Q],
-                codes[:].indirect(piece_offsets),
+                codes[:].indirect(offsets[:, first // 16 : (first + width) // 16]),
                 start=False,
                 stop=True,
             )
-            scaled = held.tile([Q, PIECE], F32, name=f"scaled{h}{p}")
+            scaled = held.tile([Q, width], F32, name=f"scaled{h}_{first}")
             if i % 2 == 0:
                 nc.vector.tensor_scalar_mul(scaled[:], bank[:], SCALE)
             else:
                 nc.scalar.activation(scaled[:], bank[:], COPY, scale=SCALE)
-            nc.sync.dma_start(out[h * Q : (h + 1) * Q, p * PIECE : (p + 1) * PIECE], scaled[:])
+            nc.sync.dma_start(out[h * Q : (h + 1) * Q, first : first + width], scaled[:])

@@ -3,14 +3,14 @@ import math
 import concourse.mybir as mybir
 
 BF16, F32, U16 = mybir.dt.bfloat16, mybir.dt.float32, mybir.dt.uint16
-COPY = mybir.ActivationFunctionType.Copy
 
 D = 128
 HEADS = 2
 Q = 128
 CODES = 1024
 N = 512
-WIDTHS = ((256, 256), (128, 128, 128, 128))
+PIECE = 256
+PIECES = N // PIECE
 SCALE = 1.0 / math.sqrt(D)
 
 FLOPS = 2 * 2 * HEADS * Q * D * N
@@ -32,29 +32,27 @@ def tile_multiheadattention_shaw_kernel(tc, table, w, keys, offs, out):
         codes = held.tile([D, CODES], BF16, name="codes")
         nc.sync.dma_start(codes[:], table)
 
-        pieces = [(h, sum(WIDTHS[h][:p]), WIDTHS[h][p]) for h in range(HEADS) for p in range(len(WIDTHS[h]))]
-        scores = [psum.tile([Q, width], F32, name=f"scores{h}_{first}") for h, first, width in pieces]
+        pieces = [(h, p) for h in range(HEADS) for p in range(PIECES)]
+        scores = [psum.tile([Q, PIECE], F32, name=f"scores{h}{p}") for h, p in pieces]
 
-        for (h, first, width), bank in zip(pieces, scores):
+        for (h, p), bank in zip(pieces, scores):
             nc.tensor.matmul(
                 bank[:],
                 queries[:, h * Q : (h + 1) * Q],
-                head_keys[h][:, first : first + width],
+                head_keys[h][:, p * PIECE : (p + 1) * PIECE],
                 start=True,
                 stop=False,
             )
 
-        for i, ((h, first, width), bank) in enumerate(zip(pieces, scores)):
+        for (h, p), bank in zip(pieces, scores):
+            piece_offsets = offsets[:, p * (PIECE // 16) : (p + 1) * (PIECE // 16)]
             nc.tensor.matmul(
                 bank[:],
                 queries[:, h * Q : (h + 1) * Q],
-                codes[:].indirect(offsets[:, first // 16 : (first + width) // 16]),
+                codes[:].indirect(piece_offsets),
                 start=False,
                 stop=True,
             )
-            scaled = held.tile([Q, width], F32, name=f"scaled{h}_{first}")
-            if i % 2 == 0:
-                nc.vector.tensor_scalar_mul(scaled[:], bank[:], SCALE)
-            else:
-                nc.scalar.activation(scaled[:], bank[:], COPY, scale=SCALE)
-            nc.sync.dma_start(out[h * Q : (h + 1) * Q, first : first + width], scaled[:])
+            scaled = held.tile([Q, PIECE], F32, name=f"scaled{h}{p}")
+            nc.vector.tensor_scalar_mul(scaled[:], bank[:], SCALE)
+            nc.sync.dma_start(out[h * Q : (h + 1) * Q, p * PIECE : (p + 1) * PIECE], scaled[:])

@@ -44,6 +44,7 @@ def tile_multiheadattention_shaw_kernel(tc, table, w, keys, offs, out):
                 stop=False,
             )
 
+        scaled = [held.tile([Q, N], F32, name=f"scaled{h}") for h in range(HEADS)]
         for (h, p), bank in zip(pieces, scores):
             piece_offsets = offsets[:, p * (PIECE // 16) : (p + 1) * (PIECE // 16)]
             nc.tensor.matmul(
@@ -53,6 +54,6 @@ def tile_multiheadattention_shaw_kernel(tc, table, w, keys, offs, out):
                 start=False,
                 stop=True,
             )
-            scaled = held.tile([Q, PIECE], F32, name=f"scaled{h}{p}")
-            nc.vector.tensor_scalar_mul(scaled[:], bank[:], SCALE)
-            nc.sync.dma_start(out[h * Q : (h + 1) * Q, p * PIECE : (p + 1) * PIECE], scaled[:])
+            nc.vector.tensor_scalar_mul(scaled[h][:, p * PIECE : (p + 1) * PIECE], bank[:], SCALE)
+            if p == PIECES - 1:
+                nc.sync.dma_start(out[h * Q : (h + 1) * Q, :], scaled[h][:])

@@ -9,7 +9,7 @@ HEADS = 2
 Q = 128
 CODES = 1024
 N = 512
-PIECE = 256
+PIECE = 128
 PIECES = N // PIECE
 SCALE = 1.0 / math.sqrt(D)
 

@@ -55,5 +55,7 @@ def tile_multiheadattention_shaw_kernel(tc, table, w, keys, offs, out):
                 stop=True,
             )
             nc.vector.tensor_scalar_mul(scaled[h][:, p * PIECE : (p + 1) * PIECE], bank[:], SCALE)
-            if p == PIECES - 1:
-                nc.sync.dma_start(out[h * Q : (h + 1) * Q, :], scaled[h][:])
+            if h == 0 and p % 2 == 1:
+                half = slice((p - 1) * PIECE, (p + 1) * PIECE)
+                nc.sync.dma_start(out[0:Q, half], scaled[0][:, half])
+        nc.sync.dma_start(out[Q : 2 * Q, :], scaled[1][:])

@@ -55,7 +55,8 @@ def tile_multiheadattention_shaw_kernel(tc, table, w, keys, offs, out):
                 stop=True,
             )
             nc.vector.tensor_scalar_mul(scaled[h][:, p * PIECE : (p + 1) * PIECE], bank[:], SCALE)
-            if h == 0 and p % 2 == 1:
-                half = slice((p - 1) * PIECE, (p + 1) * PIECE)
-                nc.sync.dma_start(out[0:Q, half], scaled[0][:, half])
+            if h == 0 and p == 0:
+                nc.sync.dma_start(out[0:Q, 0:PIECE], scaled[0][:, 0:PIECE])
+            if h == 0 and p == PIECES - 1:
+                nc.sync.dma_start(out[0:Q, PIECE:N], scaled[0][:, PIECE:N])
         nc.sync.dma_start(out[Q : 2 * Q, :], scaled[1][:])

import math

import concourse.mybir as mybir

BF16, F32, U16 = mybir.dt.bfloat16, mybir.dt.float32, mybir.dt.uint16

D = 128
HEADS = 2
Q = 128
CODES = 1024
N = 512
PIECE = 128
PIECES = N // PIECE
SCALE = 1.0 / math.sqrt(D)

FLOPS = 2 * 2 * HEADS * Q * D * N


def tile_multiheadattention_shaw_kernel(tc, table, w, keys, offs, out):
    nc = tc.nc
    with (
        tc.tile_pool(name="held", bufs=1) as held,
        tc.psum_pool(name="psum", bufs=1) as psum,
    ):
        queries = held.tile([D, HEADS * Q], BF16, name="queries")
        nc.sync.dma_start(queries[:], w)
        head_keys = [held.tile([D, N], BF16, name=f"head_keys{h}") for h in range(HEADS)]
        for h in range(HEADS):
            nc.sync.dma_start(head_keys[h][:], keys[h * D : (h + 1) * D, :])
        offsets = held.tile([D, N // 16], U16, name="offsets")
        nc.sync.dma_start(offsets[:], offs)
        codes = held.tile([D, CODES], BF16, name="codes")
        nc.sync.dma_start(codes[:], table)

        pieces = [(h, p) for h in range(HEADS) for p in range(PIECES)]
        scores = [psum.tile([Q, PIECE], F32, name=f"scores{h}{p}") for h, p in pieces]

        for (h, p), bank in zip(pieces, scores):
            nc.tensor.matmul(
                bank[:],
                queries[:, h * Q : (h + 1) * Q],
                head_keys[h][:, p * PIECE : (p + 1) * PIECE],
                start=True,
                stop=False,
            )

        scaled = [held.tile([Q, N], F32, name=f"scaled{h}") for h in range(HEADS)]
        for (h, p), bank in zip(pieces, scores):
            piece_offsets = offsets[:, p * (PIECE // 16) : (p + 1) * (PIECE // 16)]
            nc.tensor.matmul(
                bank[:],
                queries[:, h * Q : (h + 1) * Q],
                codes[:].indirect(piece_offsets),
                start=False,
                stop=True,
            )
            nc.vector.tensor_scalar_mul(scaled[h][:, p * PIECE : (p + 1) * PIECE], bank[:], SCALE)
            if h == 0 and p == 0:
                nc.sync.dma_start(out[0:Q, 0:PIECE], scaled[0][:, 0:PIECE])
            if h == 0 and p == PIECES - 1:
                nc.sync.dma_start(out[0:Q, PIECE:N], scaled[0][:, PIECE:N])
        nc.sync.dma_start(out[Q : 2 * Q, :], scaled[1][:])
